import numpy as np
import ml_dtypes


def mxq(x, axis, fmt="e4m3"):
    dtype, down = {"e4m3": (ml_dtypes.float8_e4m3fn, 7), "e5m2": (ml_dtypes.float8_e5m2, 14)}[fmt]
    v = np.moveaxis(np.asarray(x, np.float32).astype(ml_dtypes.bfloat16).astype(np.float64), axis, -1)
    blocks = v.reshape(v.shape[:-1] + (-1, 32))
    amax = np.abs(blocks).max(-1, keepdims=True)
    byte = np.maximum(np.where(amax > 0, np.frexp(amax)[1] - 1 + 127, 0) - down, 1)
    scale = np.exp2(byte - 127.0)
    codes = (blocks / scale).astype(np.float32).astype(dtype).astype(np.float64)
    return np.moveaxis((codes * scale).reshape(v.shape), -1, axis)


WIDE = False


def mx_kscale(k):
    if not WIDE:
        return np.ones(k)
    levels = np.array([10, -10, 5, -5, 0])
    if k % 512:
        return np.exp2(np.random.permutation(np.resize(levels, k // 32))).repeat(32)
    a = np.empty((k // 512, 16))
    for p in range(k // 512):
        a[p, :8] = np.random.permutation(np.resize(levels, 8))
        for g in range(8):
            far = levels[np.abs(levels - a[p, g]) >= 10]
            a[p, g + 8] = far[np.random.randint(len(far))]
    return np.exp2(a.ravel()).repeat(32)


BF16 = ml_dtypes.bfloat16


def bf(x):
    return np.asarray(x, np.float32).astype(BF16)


def f64(x):
    return np.asarray(x).astype(np.float64)


T, DIM, H, HKV, D = 512, 2048, 16, 4, 128
THETA = 10000.0
NQ, NK = H * D, HKV * D


def rope(u):
    inv_freq = 1.0 / THETA ** (np.arange(0, D, 2) / D)
    ang = np.arange(T)[:, None] * inv_freq
    cos, sin = np.cos(ang)[:, None, :], np.sin(ang)[:, None, :]
    p = u.reshape(T, -1, D // 2, 2)
    u1, u2 = p[..., 0], p[..., 1]
    return np.stack([u1 * cos - u2 * sin, u1 * sin + u2 * cos], axis=-1).reshape(u.shape)


def setup_inputs():
    s = mx_kscale(DIM)
    return {"x": bf(np.random.standard_normal((T, DIM)) * s),
            "w_qkv": bf(np.random.standard_normal((NQ + NK + NK, DIM)) / np.sqrt(DIM) / s)}


def reference(x, w_qkv):
    qkv = mxq(f64(x), 1, "e4m3") @ mxq(f64(w_qkv), 1, "e4m3").T
    q = qkv[:, :NQ].reshape(T, H, D)
    k = qkv[:, NQ:NQ + NK].reshape(T, HKV, D)
    v = qkv[:, NQ + NK:].reshape(T, HKV, D)
    return rope(q), rope(k), v

@@ -1,0 +1,221 @@
+import math
+from contextlib import ExitStack
+
+import concourse.mybir as mybir
+from concourse.masks import make_identity
+
+BF16 = mybir.dt.bfloat16
+F32 = mybir.dt.float32
+I32 = mybir.dt.int32
+U32 = mybir.dt.uint32
+U8 = mybir.dt.uint8
+FP8X4 = mybir.dt.float8_e4m3fn_x4
+ALU = mybir.AluOpType
+ACT = mybir.ActivationFunctionType
+
+P = 128
+PACK = 4
+K_PASS = P * PACK
+T, DIM, D = 512, 2048, 128
+N_FEATURES = 3072
+THETA = 10000.0
+PAIRS = D // 2
+DOUBLINGS = 6
+PASSES = DIM // K_PASS
+T_TILES = T // P
+N_TILE = 512
+HEADS = N_TILE // D
+FEATURE_TILES = N_FEATURES // N_TILE
+ROTATED_TILES = 5
+BLOCKS = N_TILE // P
+HALF = N_TILE // 2
+ROUND_TO_INTEGER = 1.5 * 2.0**23
+
+FLOPS = 2 * T * N_FEATURES * DIM
+
+
+def tile_attention_pa_kernel(tc, x, w_qkv, out_0, out_1, out_2):
+    nc = tc.nc
+    with ExitStack() as stack:
+        stack.enter_context(tc.manual_schedule())
+        const = stack.enter_context(tc.tile_pool(name="const", bufs=1))
+        rows_pool = stack.enter_context(tc.tile_pool(name="rows", bufs=1))
+        grouped_pool = stack.enter_context(tc.tile_pool(name="grouped", bufs=2))
+        codes_pool = stack.enter_context(tc.tile_pool(name="codes", bufs=2))
+        result_pool = stack.enter_context(tc.tile_pool(name="result", bufs=12))
+        partial_pool = stack.enter_context(tc.tile_pool(name="partial", bufs=4))
+        flip_psum = stack.enter_context(tc.psum_pool(name="flip", bufs=4))
+        acc_psum = stack.enter_context(tc.psum_pool(name="acc", bufs=4))
+
+        def load_rows(source, first_row, name):
+            rows = rows_pool.tile([P, DIM], BF16, name=name)
+            nc.sync.dma_start(out=rows[:], in_=source[first_row : first_row + P, :])
+            return rows
+
+        x_rows = [load_rows(x, P * j, "x_rows%d" % j) for j in range(T_TILES)]
+        w_rows = [load_rows(w_qkv, P * b, "w_rows%d" % b) for b in range(N_FEATURES // P)]
+
+        warm = const.tile([P, 1], F32)
+        nc.vector.memset(warm[:], 0.0)
+        nc.scalar.activation(out=warm[:], in_=warm[:], func=ACT.Sin)
+
+        position_int = const.tile([P, T_TILES], I32)
+        nc.gpsimd.iota(position_int[:], pattern=[[P, T_TILES]], base=0, channel_multiplier=1)
+        identity = const.tile([P, P], F32)
+        make_identity(nc, identity[:])
+        position = const.tile([P, T_TILES], F32)
+        nc.vector.tensor_copy(out=position[:], in_=position_int[:])
+
+        turns = const.tile([P, 3, T_TILES, PAIRS], F32)
+        nc.vector.tensor_scalar_mul(
+            out=turns[:, 2, :, 0:1], in0=position[:].unsqueeze(2), scalar1=1.0 / (2.0 * math.pi)
+        )
+        for doubling in range(DOUBLINGS):
+            filled = 2**doubling
+            nc.vector.tensor_scalar_mul(
+                out=turns[:, 2, :, filled : 2 * filled],
+                in0=turns[:, 2, :, 0:filled],
+                scalar1=THETA ** (-filled / PAIRS),
+            )
+        nc.vector.tensor_scalar_mul(out=turns[:, 0, :, :], in0=turns[:, 2, :, :], scalar1=-1.0)
+        nc.vector.tensor_scalar_add(out=turns[:, 1, :, :], in0=turns[:, 2, :, :], scalar1=0.25)
+        whole = const.tile([P, 3, T_TILES, PAIRS], F32)
+        nc.vector.tensor_scalar(
+            out=whole[:],
+            in0=turns[:],
+            scalar1=ROUND_TO_INTEGER,
+            scalar2=ROUND_TO_INTEGER,
+            op0=ALU.add,
+            op1=ALU.subtract,
+        )
+        part = const.tile([P, 3, T_TILES, PAIRS], F32)
+        nc.vector.tensor_sub(out=part[:], in0=turns[:], in1=whole[:])
+        trig = const.tile([P, 3, T_TILES, PAIRS], F32)
+        nc.scalar.activation(out=trig[:], in_=part[:], func=ACT.Sin, scale=2.0 * math.pi)
+
+        def new_grouped():
+            return grouped_pool.tile([P, PASSES * N_TILE * PACK], BF16, name="grouped", align_bytes=64)
+
+        def transpose_rows(rows, grouped, block, copies):
+            words = rows[:].bitcast(F32)
+            grouped_words = grouped[:].bitcast(F32).rearrange("q (g c u) -> q g c u", g=PASSES, u=2)
+            for half in range(2):
+                flipped = flip_psum.tile([P, 2, 2, P], F32, name="flipped")
+                for g in range(2):
+                    for u in range(2):
+                        first = 2 * P * (2 * half + g)
+                        nc.tensor.transpose(
+                            flipped[:, g, u, :], words[:, first + u : first + 2 * P : 2], identity[:]
+                        )
+                copies[half](
+                    out=grouped_words[:, 2 * half : 2 * half + 2, P * block : P * (block + 1), :],
+                    in_=flipped[:].rearrange("q g u r -> q g r u"),
+                )
+
+        def quantise(grouped, codes, scales, first_column, columns):
+            for g in range(PASSES):
+                first = N_TILE * g + first_column
+                nc.vector.quantize_mx(
+                    out=codes[:, first : first + columns].bitcast(FP8X4),
+                    scales=scales[:, first : first + columns],
+                    in_=grouped[:, PACK * first : PACK * (first + columns)],
+                )
+
+        x_grouped = new_grouped()
+        x_codes = const.tile([P, PASSES * T], U32, align_bytes=64)
+        x_scales = const.tile([P, PASSES * T], U8, align_bytes=64)
+        for j in range(T_TILES):
+            transpose_rows(x_rows[j], x_grouped, j, (nc.scalar.copy, nc.vector.tensor_copy))
+            if j > 0:
+                quantise(x_grouped, x_codes, x_scales, P * (j - 1), P)
+        quantise(x_grouped, x_codes, x_scales, P * (T_TILES - 1), P)
+
+        def transpose_half(n, half, grouped):
+            for block in (2 * half, 2 * half + 1):
+                transpose_rows(w_rows[BLOCKS * n + block], grouped, block, (nc.scalar.copy, nc.scalar.copy))
+
+        def new_codes():
+            w_codes = codes_pool.tile([P, PASSES * N_TILE], U32, name="w_codes", align_bytes=64)
+            w_scales = codes_pool.tile([P, PASSES * N_TILE], U8, name="w_scales", align_bytes=64)
+            return w_codes, w_scales
+
+        def multiply(w_codes, w_scales, j):
+            acc = acc_psum.tile([P, N_TILE], F32, name="acc")
+            for g in range(PASSES):
+                positions = slice(T * g + P * j, T * g + P * (j + 1))
+                features = slice(N_TILE * g, N_TILE * (g + 1))
+                nc.tensor.matmul_mx(
+                    out=acc[:],
+                    lhsT=x_codes[:, positions].bitcast(FP8X4),
+                    lhsT_scale=x_scales[:, positions],
+                    rhs=w_codes[:, features].bitcast(FP8X4),
+                    rhs_scale=w_scales[:, features],
+                    start=(g == 0),
+                    stop=(g == PASSES - 1),
+                )
+            return acc
+
+        by_pair = "p (h i e) -> p h i e"
+        shape = [P, HEADS, PAIRS, 2]
+
+        def products(acc, j):
+            pairs = acc[:].rearrange(by_pair, h=HEADS, e=2)
+            result = result_pool.tile([P, N_TILE], F32, name="result")
+            odd_term = partial_pool.tile([P, N_TILE], F32, name="odd_term")
+            for member, term in ((0, result), (1, odd_term)):
+                factors = trig[:, 1 - member : 3 - member, j, :].rearrange("p e i -> p i e")
+                nc.vector.tensor_tensor(
+                    out=term[:].rearrange(by_pair, h=HEADS, e=2),
+                    in0=pairs[:, :, :, member : member + 1].to_broadcast(shape),
+                    in1=factors.unsqueeze(1).to_broadcast(shape),
+                    op=ALU.mult,
+                )
+            return result, odd_term
+
+        def destination(n, j):
+            t_rows = slice(P * j, P * (j + 1))
+            if n < 4:
+                return out_0.rearrange("t h d -> t (h d)")[t_rows, N_TILE * n : N_TILE * (n + 1)]
+            if n == 4:
+                return out_1.rearrange("t h d -> t (h d)")[t_rows, :]
+            return out_2.rearrange("t h d -> t (h d)")[t_rows, :]
+
+        def add_and_store(n, j, result, odd_term):
+            nc.gpsimd.tensor_tensor(out=result[:], in0=result[:], in1=odd_term[:], op=ALU.add)
+            nc.sync.dma_start(out=destination(n, j), in_=result[:])
+
+        def copy_and_store(n, j, acc):
+            result = result_pool.tile([P, N_TILE], F32, name="result")
+            if j % 2 == 0:
+                nc.scalar.copy(out=result[:], in_=acc[:])
+            else:
+                nc.vector.tensor_copy(out=result[:], in_=acc[:])
+            nc.sync.dma_start(out=destination(n, j), in_=result[:])
+
+        grouped = new_grouped()
+        operand = new_codes()
+        for half in range(2):
+            transpose_half(0, half, grouped)
+            quantise(grouped, operand[0], operand[1], HALF * half, HALF)
+
+        for n in range(FEATURE_TILES):
+            more = n + 1 < FEATURE_TILES
+            if more:
+                next_grouped = new_grouped()
+                next_operand = new_codes()
+            for half in range(2):
+                if more:
+                    transpose_half(n + 1, half, next_grouped)
+                tiles = (2 * half, 2 * half + 1)
+                banks = [multiply(operand[0], operand[1], j) for j in tiles]
+                if more:
+                    quantise(next_grouped, next_operand[0], next_operand[1], HALF * half, HALF)
+                if n < ROTATED_TILES:
+                    terms = [products(acc, j) for acc, j in zip(banks, tiles)]
+                for index, j in enumerate(tiles):
+                    if n < ROTATED_TILES:
+                        add_and_store(n, j, terms[index][0], terms[index][1])
+                    else:
+                        copy_and_store(n, j, banks[index])
+            if more:
+                operand = next_operand

@@ -28,6 +28,8 @@ HEADS = N_TILE // D
 FEATURE_TILES = N_FEATURES // N_TILE
 ROTATED_TILES = 5
 BLOCKS = N_TILE // P
+BANK_WORDS = 4 * P
+SCALAR_SPLITS = 3
 HALF = N_TILE // 2
 ROUND_TO_INTEGER = 1.5 * 2.0**23
 
@@ -40,9 +42,10 @@ def tile_attention_pa_kernel(tc, x, w_qkv, out_0, out_1, out_2):
         stack.enter_context(tc.manual_schedule())
         const = stack.enter_context(tc.tile_pool(name="const", bufs=1))
         rows_pool = stack.enter_context(tc.tile_pool(name="rows", bufs=1))
+        split_pool = stack.enter_context(tc.tile_pool(name="split", bufs=6))
         grouped_pool = stack.enter_context(tc.tile_pool(name="grouped", bufs=2))
         codes_pool = stack.enter_context(tc.tile_pool(name="codes", bufs=2))
-        result_pool = stack.enter_context(tc.tile_pool(name="result", bufs=12))
+        result_pool = stack.enter_context(tc.tile_pool(name="result", bufs=11))
         partial_pool = stack.enter_context(tc.tile_pool(name="partial", bufs=4))
         flip_psum = stack.enter_context(tc.psum_pool(name="flip", bufs=4))
         acc_psum = stack.enter_context(tc.psum_pool(name="acc", bufs=4))
@@ -96,17 +99,29 @@ def tile_attention_pa_kernel(tc, x, w_qkv, out_0, out_1, out_2):
         def new_grouped():
             return grouped_pool.tile([P, PASSES * N_TILE * PACK], BF16, name="grouped", align_bytes=64)
 
-        def transpose_rows(rows, grouped, block, copies):
+        def split_words(rows, bank, copy):
+            split = split_pool.tile([P, 2 * BANK_WORDS], BF16, name="split")
+            words = rows[:].bitcast(F32)[:, BANK_WORDS * bank : BANK_WORDS * (bank + 1)]
+            copy(
+                out=split[:].bitcast(F32).rearrange("r (g u q) -> r g u q", g=2, u=2),
+                in_=words.rearrange("r (g q u) -> r g u q", g=2, u=2),
+            )
+            return split
+
+        def transpose_rows(rows, grouped, block, copies, splits=(None, None)):
             words = rows[:].bitcast(F32)
             grouped_words = grouped[:].bitcast(F32).rearrange("q (g c u) -> q g c u", g=PASSES, u=2)
             for half in range(2):
                 flipped = flip_psum.tile([P, 2, 2, P], F32, name="flipped")
                 for g in range(2):
                     for u in range(2):
-                        first = 2 * P * (2 * half + g)
-                        nc.tensor.transpose(
-                            flipped[:, g, u, :], words[:, first + u : first + 2 * P : 2], identity[:]
-                        )
+                        if splits[half] is None:
+                            first = 2 * P * (2 * half + g) + u
+                            k_words = words[:, first : first - u + 2 * P : 2]
+                        else:
+                            first = P * (2 * g + u)
+                            k_words = splits[half][:].bitcast(F32)[:, first : first + P]
+                        nc.tensor.transpose(flipped[:, g, u, :], k_words, identity[:])
                 copies[half](
                     out=grouped_words[:, 2 * half : 2 * half + 2, P * block : P * (block + 1), :],
                     in_=flipped[:].rearrange("q g u r -> q g r u"),
@@ -130,9 +145,24 @@ def tile_attention_pa_kernel(tc, x, w_qkv, out_0, out_1, out_2):
                 quantise(x_grouped, x_codes, x_scales, P * (j - 1), P)
         quantise(x_grouped, x_codes, x_scales, P * (T_TILES - 1), P)
 
+        def split_half(n, half):
+            order = [(block, bank) for block in range(2) for bank in range(2)]
+            for index, (block, bank) in enumerate(order):
+                rows = w_rows[BLOCKS * n + 2 * half + block]
+                copy = nc.scalar.copy if index < SCALAR_SPLITS else nc.vector.tensor_copy
+                splits[n, half, block, bank] = split_words(rows, bank, copy)
+
         def transpose_half(n, half, grouped):
-            for block in (2 * half, 2 * half + 1):
-                transpose_rows(w_rows[BLOCKS * n + block], grouped, block, (nc.scalar.copy, nc.scalar.copy))
+            for block in range(2):
+                transpose_rows(
+                    w_rows[BLOCKS * n + 2 * half + block],
+                    grouped,
+                    2 * half + block,
+                    (nc.scalar.copy, nc.scalar.copy),
+                    [splits.get((n, half, block, bank)) for bank in range(2)],
+                )
+
+        splits = {}
 
         def new_codes():
             w_codes = codes_pool.tile([P, PASSES * N_TILE], U32, name="w_codes", align_bytes=64)
@@ -208,6 +238,9 @@ def tile_attention_pa_kernel(tc, x, w_qkv, out_0, out_1, out_2):
                     transpose_half(n + 1, half, next_grouped)
                 tiles = (2 * half, 2 * half + 1)
                 banks = [multiply(operand[0], operand[1], j) for j in tiles]
+                ahead = 2 * n + half + 3
+                if ahead < 2 * FEATURE_TILES:
+                    split_half(ahead // 2, ahead % 2)
                 if more:
                     quantise(next_grouped, next_operand[0], next_operand[1], HALF * half, HALF)
                 if n < ROTATED_TILES:

@@ -149,8 +149,8 @@ def tile_attention_pa_kernel(tc, x, w_qkv, out_0, out_1, out_2):
             order = [(block, bank) for block in range(2) for bank in range(2)]
             for index, (block, bank) in enumerate(order):
                 rows = w_rows[BLOCKS * n + 2 * half + block]
-                copy = nc.scalar.copy if index < SCALAR_SPLITS else nc.vector.tensor_copy
-                splits[n, half, block, bank] = split_words(rows, bank, copy)
+                if index < SCALAR_SPLITS:
+                    splits[n, half, block, bank] = split_words(rows, bank, nc.scalar.copy)
 
         def transpose_half(n, half, grouped):
             for block in range(2):

@@ -137,8 +137,8 @@ def tile_attention_pa_kernel(tc, x, w_qkv, out_0, out_1, out_2):
                 )
 
         x_grouped = new_grouped()
-        x_codes = const.tile([P, PASSES * T], U32, align_bytes=64)
-        x_scales = const.tile([P, PASSES * T], U8, align_bytes=64)
+        x_codes = const.tile([P, PASSES * T], U32, align_bytes=256)
+        x_scales = const.tile([P, PASSES * T], U8, align_bytes=256)
         for j in range(T_TILES):
             transpose_rows(x_rows[j], x_grouped, j, (nc.scalar.copy, nc.vector.tensor_copy))
             if j > 0:
@@ -165,8 +165,8 @@ def tile_attention_pa_kernel(tc, x, w_qkv, out_0, out_1, out_2):
         splits = {}
 
         def new_codes():
-            w_codes = codes_pool.tile([P, PASSES * N_TILE], U32, name="w_codes", align_bytes=64)
-            w_scales = codes_pool.tile([P, PASSES * N_TILE], U8, name="w_scales", align_bytes=64)
+            w_codes = codes_pool.tile([P, PASSES * N_TILE], U32, name="w_codes", align_bytes=256)
+            w_scales = codes_pool.tile([P, PASSES * N_TILE], U8, name="w_scales", align_bytes=256)
             return w_codes, w_scales
 
         def multiply(w_codes, w_scales, j):
@@ -220,7 +220,7 @@ def tile_attention_pa_kernel(tc, x, w_qkv, out_0, out_1, out_2):
                 nc.scalar.copy(out=result[:], in_=acc[:])
             else:
                 nc.vector.tensor_copy(out=result[:], in_=acc[:])
-            nc.sync.dma_start(out=destination(n, j), in_=result[:])
+            nc.scalar.dma_start(out=destination(n, j), in_=result[:])
 
         grouped = new_grouped()
         operand = new_codes()

@@ -28,9 +28,11 @@ HEADS = N_TILE // D
 FEATURE_TILES = N_FEATURES // N_TILE
 ROTATED_TILES = 5
 BLOCKS = N_TILE // P
+HALF = N_TILE // 2
+HALF_TILES = 2 * FEATURE_TILES
 BANK_WORDS = 4 * P
 SCALAR_SPLITS = 3
-HALF = N_TILE // 2
+SPLIT_LEAD = 3
 ROUND_TO_INTEGER = 1.5 * 2.0**23
 
 FLOPS = 2 * T * N_FEATURES * DIM
@@ -43,7 +45,8 @@ def tile_attention_pa_kernel(tc, x, w_qkv, out_0, out_1, out_2):
         const = stack.enter_context(tc.tile_pool(name="const", bufs=1))
         rows_pool = stack.enter_context(tc.tile_pool(name="rows", bufs=1))
         split_pool = stack.enter_context(tc.tile_pool(name="split", bufs=6))
-        grouped_pool = stack.enter_context(tc.tile_pool(name="grouped", bufs=2))
+        block_pool = stack.enter_context(tc.tile_pool(name="block", bufs=4))
+        grouped_pool = stack.enter_context(tc.tile_pool(name="grouped", bufs=3))
         codes_pool = stack.enter_context(tc.tile_pool(name="codes", bufs=2))
         result_pool = stack.enter_context(tc.tile_pool(name="result", bufs=11))
         partial_pool = stack.enter_context(tc.tile_pool(name="partial", bufs=4))
@@ -69,20 +72,19 @@ def tile_attention_pa_kernel(tc, x, w_qkv, out_0, out_1, out_2):
         position = const.tile([P, T_TILES], F32)
         nc.vector.tensor_copy(out=position[:], in_=position_int[:])
 
-        turns = const.tile([P, 3, T_TILES, PAIRS], F32)
+        turns = const.tile([P, 2, T_TILES, PAIRS], F32)
         nc.vector.tensor_scalar_mul(
-            out=turns[:, 2, :, 0:1], in0=position[:].unsqueeze(2), scalar1=1.0 / (2.0 * math.pi)
+            out=turns[:, 1, :, 0:1], in0=position[:].unsqueeze(2), scalar1=1.0 / (2.0 * math.pi)
         )
         for doubling in range(DOUBLINGS):
             filled = 2**doubling
             nc.vector.tensor_scalar_mul(
-                out=turns[:, 2, :, filled : 2 * filled],
-                in0=turns[:, 2, :, 0:filled],
+                out=turns[:, 1, :, filled : 2 * filled],
+                in0=turns[:, 1, :, 0:filled],
                 scalar1=THETA ** (-filled / PAIRS),
             )
-        nc.vector.tensor_scalar_mul(out=turns[:, 0, :, :], in0=turns[:, 2, :, :], scalar1=-1.0)
-        nc.vector.tensor_scalar_add(out=turns[:, 1, :, :], in0=turns[:, 2, :, :], scalar1=0.25)
-        whole = const.tile([P, 3, T_TILES, PAIRS], F32)
+        nc.vector.tensor_scalar_add(out=turns[:, 0, :, :], in0=turns[:, 1, :, :], scalar1=0.25)
+        whole = const.tile([P, 2, T_TILES, PAIRS], F32)
         nc.vector.tensor_scalar(
             out=whole[:],
             in0=turns[:],
@@ -91,18 +93,26 @@ def tile_attention_pa_kernel(tc, x, w_qkv, out_0, out_1, out_2):
             op0=ALU.add,
             op1=ALU.subtract,
         )
-        part = const.tile([P, 3, T_TILES, PAIRS], F32)
-        nc.vector.tensor_sub(out=part[:], in0=turns[:], in1=whole[:])
+        fraction = const.tile([P, 2, T_TILES, PAIRS], F32)
+        nc.vector.tensor_sub(out=fraction[:], in0=turns[:], in1=whole[:])
         trig = const.tile([P, 3, T_TILES, PAIRS], F32)
-        nc.scalar.activation(out=trig[:], in_=part[:], func=ACT.Sin, scale=2.0 * math.pi)
+
+        def finish_table():
+            nc.scalar.activation(out=trig[:, 1:3, :, :], in_=fraction[:], func=ACT.Sin, scale=2.0 * math.pi)
+            nc.gpsimd.tensor_scalar(
+                out=trig[:, 0, :, :], in0=trig[:, 2, :, :], scalar1=-1.0, scalar2=0.0, op0=ALU.mult, op1=ALU.add
+            )
+
+        def new_block():
+            return block_pool.tile([P, PASSES * P * PACK], BF16, name="block", align_bytes=64)
 
         def new_grouped():
-            return grouped_pool.tile([P, PASSES * N_TILE * PACK], BF16, name="grouped", align_bytes=64)
+            return grouped_pool.tile([P, PASSES * HALF * PACK], BF16, name="grouped", align_bytes=64)
 
-        def split_words(rows, bank, copy):
+        def split_words(rows, bank):
             split = split_pool.tile([P, 2 * BANK_WORDS], BF16, name="split")
             words = rows[:].bitcast(F32)[:, BANK_WORDS * bank : BANK_WORDS * (bank + 1)]
-            copy(
+            nc.scalar.copy(
                 out=split[:].bitcast(F32).rearrange("r (g u q) -> r g u q", g=2, u=2),
                 in_=words.rearrange("r (g q u) -> r g u q", g=2, u=2),
             )
@@ -111,71 +121,69 @@ def tile_attention_pa_kernel(tc, x, w_qkv, out_0, out_1, out_2):
         def transpose_rows(rows, grouped, block, copies, splits=(None, None)):
             words = rows[:].bitcast(F32)
             grouped_words = grouped[:].bitcast(F32).rearrange("q (g c u) -> q g c u", g=PASSES, u=2)
-            for half in range(2):
+            for bank in range(2):
                 flipped = flip_psum.tile([P, 2, 2, P], F32, name="flipped")
                 for g in range(2):
                     for u in range(2):
-                        if splits[half] is None:
-                            first = 2 * P * (2 * half + g) + u
+                        if splits[bank] is None:
+                            first = 2 * P * (2 * bank + g) + u
                             k_words = words[:, first : first - u + 2 * P : 2]
                         else:
                             first = P * (2 * g + u)
-                            k_words = splits[half][:].bitcast(F32)[:, first : first + P]
+                            k_words = splits[bank][:].bitcast(F32)[:, first : first + P]
                         nc.tensor.transpose(flipped[:, g, u, :], k_words, identity[:])
-                copies[half](
-                    out=grouped_words[:, 2 * half : 2 * half + 2, P * block : P * (block + 1), :],
+                copies[bank](
+                    out=grouped_words[:, 2 * bank : 2 * bank + 2, P * block : P * (block + 1), :],
                     in_=flipped[:].rearrange("q g u r -> q g r u"),
                 )
 
-        def quantise(grouped, codes, scales, first_column, columns):
+        def quantise(grouped, width, codes, scales, first_code):
             for g in range(PASSES):
-                first = N_TILE * g + first_column
+                first = N_TILE * g + first_code
                 nc.vector.quantize_mx(
-                    out=codes[:, first : first + columns].bitcast(FP8X4),
-                    scales=scales[:, first : first + columns],
-                    in_=grouped[:, PACK * first : PACK * (first + columns)],
+                    out=codes[:, first : first + width].bitcast(FP8X4),
+                    scales=scales[:, first : first + width],
+                    in_=grouped[:, PACK * width * g : PACK * width * (g + 1)],
                 )
 
-        x_grouped = new_grouped()
         x_codes = const.tile([P, PASSES * T], U32, align_bytes=256)
         x_scales = const.tile([P, PASSES * T], U8, align_bytes=256)
+        x_blocks = []
         for j in range(T_TILES):
-            transpose_rows(x_rows[j], x_grouped, j, (nc.scalar.copy, nc.vector.tensor_copy))
-            if j > 0:
-                quantise(x_grouped, x_codes, x_scales, P * (j - 1), P)
-        quantise(x_grouped, x_codes, x_scales, P * (T_TILES - 1), P)
-
-        def split_half(n, half):
-            order = [(block, bank) for block in range(2) for bank in range(2)]
-            for index, (block, bank) in enumerate(order):
-                rows = w_rows[BLOCKS * n + 2 * half + block]
-                if index < SCALAR_SPLITS:
-                    splits[n, half, block, bank] = split_words(rows, bank, nc.scalar.copy)
-
-        def transpose_half(n, half, grouped):
-            for block in range(2):
-                transpose_rows(
-                    w_rows[BLOCKS * n + 2 * half + block],
-                    grouped,
-                    2 * half + block,
-                    (nc.scalar.copy, nc.scalar.copy),
-                    [splits.get((n, half, block, bank)) for bank in range(2)],
-                )
+            x_blocks.append(new_block())
+            transpose_rows(x_rows[j], x_blocks[j], 0, (nc.scalar.copy, nc.vector.tensor_copy))
+            if j == 0:
+                finish_table()
+            else:
+                quantise(x_blocks[j - 1], P, x_codes, x_scales, P * (j - 1))
+        quantise(x_blocks[T_TILES - 1], P, x_codes, x_scales, P * (T_TILES - 1))
 
         splits = {}
+
+        def split_half(half_tile):
+            order = [(block, bank) for block in range(2) for bank in range(2)]
+            for block, bank in order[:SCALAR_SPLITS]:
+                splits[half_tile, block, bank] = split_words(w_rows[2 * half_tile + block], bank)
+
+        def transpose_half(half_tile, grouped):
+            for block in range(2):
+                sorted_words = [splits.get((half_tile, block, bank)) for bank in range(2)]
+                rows = w_rows[2 * half_tile + block]
+                transpose_rows(rows, grouped, block, (nc.scalar.copy, nc.scalar.copy), sorted_words)
 
         def new_codes():
             w_codes = codes_pool.tile([P, PASSES * N_TILE], U32, name="w_codes", align_bytes=256)
             w_scales = codes_pool.tile([P, PASSES * N_TILE], U8, name="w_scales", align_bytes=256)
             return w_codes, w_scales
 
-        def multiply(w_codes, w_scales, j):
+        def multiply(operand, j, first=0, width=N_TILE):
+            w_codes, w_scales = operand
             acc = acc_psum.tile([P, N_TILE], F32, name="acc")
             for g in range(PASSES):
                 positions = slice(T * g + P * j, T * g + P * (j + 1))
-                features = slice(N_TILE * g, N_TILE * (g + 1))
+                features = slice(N_TILE * g + first, N_TILE * g + first + width)
                 nc.tensor.matmul_mx(
-                    out=acc[:],
+                    out=acc[:, 0:width],
                     lhsT=x_codes[:, positions].bitcast(FP8X4),
                     lhsT_scale=x_scales[:, positions],
                     rhs=w_codes[:, features].bitcast(FP8X4),
@@ -211,44 +219,45 @@ def tile_attention_pa_kernel(tc, x, w_qkv, out_0, out_1, out_2):
             return out_2.rearrange("t h d -> t (h d)")[t_rows, :]
 
         def add_and_store(n, j, result, odd_term):
-            nc.gpsimd.tensor_tensor(out=result[:], in0=result[:], in1=odd_term[:], op=ALU.add)
+            adder = nc.vector if n == ROTATED_TILES - 1 and j >= 2 else nc.gpsimd
+            adder.tensor_tensor(out=result[:], in0=result[:], in1=odd_term[:], op=ALU.add)
             nc.sync.dma_start(out=destination(n, j), in_=result[:])
 
-        def copy_and_store(n, j, acc):
+        def copy_and_store(copy, queue, acc, target, width=N_TILE):
             result = result_pool.tile([P, N_TILE], F32, name="result")
-            if j % 2 == 0:
-                nc.scalar.copy(out=result[:], in_=acc[:])
-            else:
-                nc.vector.tensor_copy(out=result[:], in_=acc[:])
-            nc.scalar.dma_start(out=destination(n, j), in_=result[:])
+            copy(out=result[:, 0:width], in_=acc[:, 0:width])
+            queue.dma_start(out=target, in_=result[:, 0:width])
 
-        grouped = new_grouped()
         operand = new_codes()
-        for half in range(2):
-            transpose_half(0, half, grouped)
-            quantise(grouped, operand[0], operand[1], HALF * half, HALF)
+        w_blocks = []
+        for block in range(BLOCKS):
+            w_blocks.append(new_block())
+            second_copy = nc.vector.tensor_copy if block % 2 == 1 else nc.scalar.copy
+            transpose_rows(w_rows[block], w_blocks[block], 0, (nc.scalar.copy, second_copy))
+            if block > 0:
+                quantise(w_blocks[block - 1], P, *operand, P * (block - 1))
+        quantise(w_blocks[BLOCKS - 1], P, *operand, P * (BLOCKS - 1))
 
-        for n in range(FEATURE_TILES):
-            more = n + 1 < FEATURE_TILES
-            if more:
-                next_grouped = new_grouped()
-                next_operand = new_codes()
+        for n in range(ROTATED_TILES):
+            next_operand = new_codes()
             for half in range(2):
-                if more:
-                    transpose_half(n + 1, half, next_grouped)
+                grouped = new_grouped()
+                transpose_half(2 * (n + 1) + half, grouped)
                 tiles = (2 * half, 2 * half + 1)
-                banks = [multiply(operand[0], operand[1], j) for j in tiles]
-                ahead = 2 * n + half + 3
-                if ahead < 2 * FEATURE_TILES:
-                    split_half(ahead // 2, ahead % 2)
-                if more:
-                    quantise(next_grouped, next_operand[0], next_operand[1], HALF * half, HALF)
-                if n < ROTATED_TILES:
-                    terms = [products(acc, j) for acc, j in zip(banks, tiles)]
-                for index, j in enumerate(tiles):
-                    if n < ROTATED_TILES:
-                        add_and_store(n, j, terms[index][0], terms[index][1])
-                    else:
-                        copy_and_store(n, j, banks[index])
-            if more:
-                operand = next_operand
+                banks = [multiply(operand, j) for j in tiles]
+                ahead = 2 * n + half + SPLIT_LEAD
+                if ahead < HALF_TILES:
+                    split_half(ahead)
+                quantise(grouped, HALF, *next_operand, HALF * half)
+                terms = [products(acc, j) for acc, j in zip(banks, tiles)]
+                for j, (result, odd_term) in zip(tiles, terms):
+                    add_and_store(n, j, result, odd_term)
+            operand = next_operand
+
+        n = ROTATED_TILES
+        for j in range(T_TILES - 1):
+            copy_and_store(nc.scalar.copy, nc.scalar, multiply(operand, j), destination(n, j))
+        j = T_TILES - 1
+        for first, copy, queue in ((0, nc.vector.tensor_copy, nc.sync), (HALF, nc.scalar.copy, nc.scalar)):
+            acc = multiply(operand, j, first, HALF)
+            copy_and_store(copy, queue, acc, destination(n, j)[:, first : first + HALF], HALF)

import math
from contextlib import ExitStack

import concourse.mybir as mybir
from concourse.masks import make_identity

BF16 = mybir.dt.bfloat16
F32 = mybir.dt.float32
I32 = mybir.dt.int32
U32 = mybir.dt.uint32
U8 = mybir.dt.uint8
FP8X4 = mybir.dt.float8_e4m3fn_x4
ALU = mybir.AluOpType
ACT = mybir.ActivationFunctionType

P = 128
PACK = 4
K_PASS = P * PACK
T, DIM, D = 512, 2048, 128
N_FEATURES = 3072
THETA = 10000.0
PAIRS = D // 2
DOUBLINGS = 6
PASSES = DIM // K_PASS
T_TILES = T // P
N_TILE = 512
HEADS = N_TILE // D
FEATURE_TILES = N_FEATURES // N_TILE
ROTATED_TILES = 5
BLOCKS = N_TILE // P
HALF = N_TILE // 2
HALF_TILES = 2 * FEATURE_TILES
BANK_WORDS = 4 * P
SCALAR_SPLITS = 3
SPLIT_LEAD = 3
ROUND_TO_INTEGER = 1.5 * 2.0**23

FLOPS = 2 * T * N_FEATURES * DIM


def tile_attention_pa_kernel(tc, x, w_qkv, out_0, out_1, out_2):
    nc = tc.nc
    with ExitStack() as stack:
        stack.enter_context(tc.manual_schedule())
        const = stack.enter_context(tc.tile_pool(name="const", bufs=1))
        rows_pool = stack.enter_context(tc.tile_pool(name="rows", bufs=1))
        split_pool = stack.enter_context(tc.tile_pool(name="split", bufs=6))
        block_pool = stack.enter_context(tc.tile_pool(name="block", bufs=4))
        grouped_pool = stack.enter_context(tc.tile_pool(name="grouped", bufs=3))
        codes_pool = stack.enter_context(tc.tile_pool(name="codes", bufs=2))
        result_pool = stack.enter_context(tc.tile_pool(name="result", bufs=11))
        partial_pool = stack.enter_context(tc.tile_pool(name="partial", bufs=4))
        flip_psum = stack.enter_context(tc.psum_pool(name="flip", bufs=4))
        acc_psum = stack.enter_context(tc.psum_pool(name="acc", bufs=4))

        def load_rows(source, first_row, name):
            rows = rows_pool.tile([P, DIM], BF16, name=name)
            nc.sync.dma_start(out=rows[:], in_=source[first_row : first_row + P, :])
            return rows

        x_rows = [load_rows(x, P * j, "x_rows%d" % j) for j in range(T_TILES)]
        w_rows = [load_rows(w_qkv, P * b, "w_rows%d" % b) for b in range(N_FEATURES // P)]

        warm = const.tile([P, 1], F32)
        nc.vector.memset(warm[:], 0.0)
        nc.scalar.activation(out=warm[:], in_=warm[:], func=ACT.Sin)

        position_int = const.tile([P, T_TILES], I32)
        nc.gpsimd.iota(position_int[:], pattern=[[P, T_TILES]], base=0, channel_multiplier=1)
        identity = const.tile([P, P], F32)
        make_identity(nc, identity[:])
        position = const.tile([P, T_TILES], F32)
        nc.vector.tensor_copy(out=position[:], in_=position_int[:])

        turns = const.tile([P, 2, T_TILES, PAIRS], F32)
        nc.vector.tensor_scalar_mul(
            out=turns[:, 1, :, 0:1], in0=position[:].unsqueeze(2), scalar1=1.0 / (2.0 * math.pi)
        )
        for doubling in range(DOUBLINGS):
            filled = 2**doubling
            nc.vector.tensor_scalar_mul(
                out=turns[:, 1, :, filled : 2 * filled],
                in0=turns[:, 1, :, 0:filled],
                scalar1=THETA ** (-filled / PAIRS),
            )
        nc.vector.tensor_scalar_add(out=turns[:, 0, :, :], in0=turns[:, 1, :, :], scalar1=0.25)
        whole = const.tile([P, 2, T_TILES, PAIRS], F32)
        nc.vector.tensor_scalar(
            out=whole[:],
            in0=turns[:],
            scalar1=ROUND_TO_INTEGER,
            scalar2=ROUND_TO_INTEGER,
            op0=ALU.add,
            op1=ALU.subtract,
        )
        fraction = const.tile([P, 2, T_TILES, PAIRS], F32)
        nc.vector.tensor_sub(out=fraction[:], in0=turns[:], in1=whole[:])
        trig = const.tile([P, 3, T_TILES, PAIRS], F32)

        def finish_table():
            nc.scalar.activation(out=trig[:, 1:3, :, :], in_=fraction[:], func=ACT.Sin, scale=2.0 * math.pi)
            nc.gpsimd.tensor_scalar(
                out=trig[:, 0, :, :], in0=trig[:, 2, :, :], scalar1=-1.0, scalar2=0.0, op0=ALU.mult, op1=ALU.add
            )

        def new_block():
            return block_pool.tile([P, PASSES * P * PACK], BF16, name="block", align_bytes=64)

        def new_grouped():
            return grouped_pool.tile([P, PASSES * HALF * PACK], BF16, name="grouped", align_bytes=64)

        def split_words(rows, bank):
            split = split_pool.tile([P, 2 * BANK_WORDS], BF16, name="split")
            words = rows[:].bitcast(F32)[:, BANK_WORDS * bank : BANK_WORDS * (bank + 1)]
            nc.scalar.copy(
                out=split[:].bitcast(F32).rearrange("r (g u q) -> r g u q", g=2, u=2),
                in_=words.rearrange("r (g q u) -> r g u q", g=2, u=2),
            )
            return split

        def transpose_rows(rows, grouped, block, copies, splits=(None, None)):
            words = rows[:].bitcast(F32)
            grouped_words = grouped[:].bitcast(F32).rearrange("q (g c u) -> q g c u", g=PASSES, u=2)
            for bank in range(2):
                flipped = flip_psum.tile([P, 2, 2, P], F32, name="flipped")
                for g in range(2):
                    for u in range(2):
                        if splits[bank] is None:
                            first = 2 * P * (2 * bank + g) + u
                            k_words = words[:, first : first - u + 2 * P : 2]
                        else:
                            first = P * (2 * g + u)
                            k_words = splits[bank][:].bitcast(F32)[:, first : first + P]
                        nc.tensor.transpose(flipped[:, g, u, :], k_words, identity[:])
                copies[bank](
                    out=grouped_words[:, 2 * bank : 2 * bank + 2, P * block : P * (block + 1), :],
                    in_=flipped[:].rearrange("q g u r -> q g r u"),
                )

        def quantise(grouped, width, codes, scales, first_code):
            for g in range(PASSES):
                first = N_TILE * g + first_code
                nc.vector.quantize_mx(
                    out=codes[:, first : first + width].bitcast(FP8X4),
                    scales=scales[:, first : first + width],
                    in_=grouped[:, PACK * width * g : PACK * width * (g + 1)],
                )

        x_codes = const.tile([P, PASSES * T], U32, align_bytes=256)
        x_scales = const.tile([P, PASSES * T], U8, align_bytes=256)
        x_blocks = []
        for j in range(T_TILES):
            x_blocks.append(new_block())
            transpose_rows(x_rows[j], x_blocks[j], 0, (nc.scalar.copy, nc.vector.tensor_copy))
            if j == 0:
                finish_table()
            else:
                quantise(x_blocks[j - 1], P, x_codes, x_scales, P * (j - 1))
        quantise(x_blocks[T_TILES - 1], P, x_codes, x_scales, P * (T_TILES - 1))

        splits = {}

        def split_half(half_tile):
            order = [(block, bank) for block in range(2) for bank in range(2)]
            for block, bank in order[:SCALAR_SPLITS]:
                splits[half_tile, block, bank] = split_words(w_rows[2 * half_tile + block], bank)

        def transpose_half(half_tile, grouped):
            for block in range(2):
                sorted_words = [splits.get((half_tile, block, bank)) for bank in range(2)]
                rows = w_rows[2 * half_tile + block]
                transpose_rows(rows, grouped, block, (nc.scalar.copy, nc.scalar.copy), sorted_words)

        def new_codes():
            w_codes = codes_pool.tile([P, PASSES * N_TILE], U32, name="w_codes", align_bytes=256)
            w_scales = codes_pool.tile([P, PASSES * N_TILE], U8, name="w_scales", align_bytes=256)
            return w_codes, w_scales

        def multiply(operand, j, first=0, width=N_TILE):
            w_codes, w_scales = operand
            acc = acc_psum.tile([P, N_TILE], F32, name="acc")
            for g in range(PASSES):
                positions = slice(T * g + P * j, T * g + P * (j + 1))
                features = slice(N_TILE * g + first, N_TILE * g + first + width)
                nc.tensor.matmul_mx(
                    out=acc[:, 0:width],
                    lhsT=x_codes[:, positions].bitcast(FP8X4),
                    lhsT_scale=x_scales[:, positions],
                    rhs=w_codes[:, features].bitcast(FP8X4),
                    rhs_scale=w_scales[:, features],
                    start=(g == 0),
                    stop=(g == PASSES - 1),
                )
            return acc

        by_pair = "p (h i e) -> p h i e"
        shape = [P, HEADS, PAIRS, 2]

        def products(acc, j):
            pairs = acc[:].rearrange(by_pair, h=HEADS, e=2)
            result = result_pool.tile([P, N_TILE], F32, name="result")
            odd_term = partial_pool.tile([P, N_TILE], F32, name="odd_term")
            for member, term in ((0, result), (1, odd_term)):
                factors = trig[:, 1 - member : 3 - member, j, :].rearrange("p e i -> p i e")
                nc.vector.tensor_tensor(
                    out=term[:].rearrange(by_pair, h=HEADS, e=2),
                    in0=pairs[:, :, :, member : member + 1].to_broadcast(shape),
                    in1=factors.unsqueeze(1).to_broadcast(shape),
                    op=ALU.mult,
                )
            return result, odd_term

        def destination(n, j):
            t_rows = slice(P * j, P * (j + 1))
            if n < 4:
                return out_0.rearrange("t h d -> t (h d)")[t_rows, N_TILE * n : N_TILE * (n + 1)]
            if n == 4:
                return out_1.rearrange("t h d -> t (h d)")[t_rows, :]
            return out_2.rearrange("t h d -> t (h d)")[t_rows, :]

        def add_and_store(n, j, result, odd_term):
            adder = nc.vector if n == ROTATED_TILES - 1 and j >= 2 else nc.gpsimd
            adder.tensor_tensor(out=result[:], in0=result[:], in1=odd_term[:], op=ALU.add)
            nc.sync.dma_start(out=destination(n, j), in_=result[:])

        def copy_and_store(copy, queue, acc, target, width=N_TILE):
            result = result_pool.tile([P, N_TILE], F32, name="result")
            copy(out=result[:, 0:width], in_=acc[:, 0:width])
            queue.dma_start(out=target, in_=result[:, 0:width])

        operand = new_codes()
        w_blocks = []
        for block in range(BLOCKS):
            w_blocks.append(new_block())
            second_copy = nc.vector.tensor_copy if block % 2 == 1 else nc.scalar.copy
            transpose_rows(w_rows[block], w_blocks[block], 0, (nc.scalar.copy, second_copy))
            if block > 0:
                quantise(w_blocks[block - 1], P, *operand, P * (block - 1))
        quantise(w_blocks[BLOCKS - 1], P, *operand, P * (BLOCKS - 1))

        for n in range(ROTATED_TILES):
            next_operand = new_codes()
            for half in range(2):
                grouped = new_grouped()
                transpose_half(2 * (n + 1) + half, grouped)
                tiles = (2 * half, 2 * half + 1)
                banks = [multiply(operand, j) for j in tiles]
                ahead = 2 * n + half + SPLIT_LEAD
                if ahead < HALF_TILES:
                    split_half(ahead)
                quantise(grouped, HALF, *next_operand, HALF * half)
                terms = [products(acc, j) for acc, j in zip(banks, tiles)]
                for j, (result, odd_term) in zip(tiles, terms):
                    add_and_store(n, j, result, odd_term)
            operand = next_operand

        n = ROTATED_TILES
        for j in range(T_TILES - 1):
            copy_and_store(nc.scalar.copy, nc.scalar, multiply(operand, j), destination(n, j))
        j = T_TILES - 1
        for first, copy, queue in ((0, nc.vector.tensor_copy, nc.sync), (HALF, nc.scalar.copy, nc.scalar)):
            acc = multiply(operand, j, first, HALF)
            copy_and_store(copy, queue, acc, destination(n, j)[:, first : first + HALF], HALF)
